import numpy as np
import ml_dtypes


def mxq(x, axis, fmt="e4m3"):
    dtype, down = {"e4m3": (ml_dtypes.float8_e4m3fn, 7), "e5m2": (ml_dtypes.float8_e5m2, 14)}[fmt]
    v = np.moveaxis(np.asarray(x, np.float32).astype(ml_dtypes.bfloat16).astype(np.float64), axis, -1)
    blocks = v.reshape(v.shape[:-1] + (-1, 32))
    amax = np.abs(blocks).max(-1, keepdims=True)
    byte = np.maximum(np.where(amax > 0, np.frexp(amax)[1] - 1 + 127, 0) - down, 1)
    scale = np.exp2(byte - 127.0)
    codes = (blocks / scale).astype(np.float32).astype(dtype).astype(np.float64)
    return np.moveaxis((codes * scale).reshape(v.shape), -1, axis)


WIDE = False


def mx_kscale(k):
    if not WIDE:
        return np.ones(k)
    levels = np.array([10, -10, 5, -5, 0])
    a = np.random.permutation(np.resize(levels, k // 512 * 4)).reshape(k // 512, 4)
    idx = np.arange(k)
    return np.exp2(a[idx // 512, idx % 128 // 32])


BF16 = ml_dtypes.bfloat16


def bf(x):
    return np.asarray(x, np.float32).astype(BF16)


def f64(x):
    return np.asarray(x).astype(np.float64)


B, S, D, H, DN, DR, DV, RQ, RKV = 2, 256, 2048, 16, 64, 128, 128, 1536, 512
THETA = 10000.0
EPS = 1e-6


def rmsnorm(v, w):
    return v * (1.0 / np.sqrt(np.mean(v * v, axis=-1, keepdims=True) + EPS)) * w


def rotate_half(v):
    v1 = v[..., ::2]
    v2 = v[..., 1::2]
    return np.stack((-v2, v1), axis=-1).reshape(v.shape)


def rope_cache():
    inv_freq = 1.0 / THETA ** (np.arange(0, DR, 2) / DR)
    freqs = np.outer(np.arange(S), inv_freq)
    emb = np.concatenate((freqs, freqs), -1)
    return np.cos(emb), np.sin(emb)


def apply_rope(v, cos, sin):
    return v * cos[None, None] + rotate_half(v) * sin[None, None]


def setup_inputs():
    s, t = mx_kscale(D), mx_kscale(RQ)
    return {"x": bf(np.random.standard_normal((B, S, D)) * s),
            "Wqa": bf(np.random.standard_normal((D, RQ)) / np.sqrt(D) / s[:, None]),
            "q_a_norm_w": bf((1.0 + 0.1 * np.random.standard_normal(RQ)) * t),
            "Wqb": bf(np.random.standard_normal((RQ, H * (DN + DR))) / np.sqrt(RQ) / t[:, None])}


def reference(x, Wqa, q_a_norm_w, Wqb):
    c = mxq(f64(x), 2, "e4m3") @ mxq(f64(Wqa), 0, "e4m3")
    h = rmsnorm(c, f64(q_a_norm_w))
    q = mxq(h, 2, "e4m3") @ mxq(f64(Wqb), 0, "e4m3")
    q = q.reshape(B, S, H, DN + DR).transpose(0, 2, 1, 3)
    q_nope, q_rope = q[..., :DN], q[..., DN:]
    cos, sin = rope_cache()
    q_rope = apply_rope(q_rope, cos, sin)
    return np.concatenate([q_nope, q_rope], -1)

@@ -1,0 +1,362 @@
+from contextlib import ExitStack
+import math
+
+import concourse.mybir as mybir
+from concourse.masks import make_identity
+
+F32 = mybir.dt.float32
+BF16 = mybir.dt.bfloat16
+I32 = mybir.dt.int32
+U32 = mybir.dt.uint32
+U8 = mybir.dt.uint8
+FP8X4 = mybir.dt.float8_e4m3fn_x4
+ALU = mybir.AluOpType
+ACT = mybir.ActivationFunctionType
+
+P = 128
+PACK = 4
+K_PASS = P * PACK
+BANK = 512
+
+BATCH, SEQ, D_MODEL, HEADS, D_NOPE, D_ROPE, RANK = 2, 256, 2048, 16, 64, 128, 1536
+D_HEAD = D_NOPE + D_ROPE
+THETA = 10000.0
+EPS = 1e-6
+N_FREQ = D_ROPE // 2
+
+TOK_TILES = BATCH * SEQ // P
+SEQ_TILES = SEQ // P
+X_PASSES = D_MODEL // K_PASS
+H_PASSES = RANK // K_PASS
+RANK_BANKS = RANK // BANK
+GROUP_HEADS = 4
+GROUPS = HEADS // GROUP_HEADS
+LOAD_COLS = 1536
+ROUND_MAGIC = 12582912.0
+
+FLOPS = 2 * BATCH * SEQ * (D_MODEL * RANK + RANK * HEADS * D_HEAD)
+
+
+def regroup(copy, grouped, rows):
+    copy(
+        out=grouped.rearrange("p (n c i) t -> p n c t i", n=rows.shape[2], i=4),
+        in_=rows.rearrange("p t n (c i) -> p n c t i", i=4),
+    )
+
+
+def build_rope_tables(nc, const):
+    position_int = const.tile([P, SEQ_TILES], I32)
+    nc.gpsimd.iota(position_int[:], pattern=[[P, SEQ_TILES]], base=0, channel_multiplier=1)
+    position = const.tile([P, SEQ_TILES], F32)
+    nc.vector.tensor_copy(out=position[:], in_=position_int[:])
+
+    freq = const.tile([P, N_FREQ], F32)
+    nc.vector.memset(freq[:, 0:1], 1.0)
+    for level in range(6):
+        span = 1 << level
+        nc.vector.tensor_scalar(
+            out=freq[:, span : 2 * span],
+            in0=freq[:, 0:span],
+            scalar1=THETA ** (-span / N_FREQ),
+            scalar2=None,
+            op0=ALU.mult,
+        )
+
+    turns = const.tile([P, 2, SEQ_TILES, N_FREQ], F32)
+    for a in range(SEQ_TILES):
+        nc.vector.tensor_scalar(
+            out=turns[:, 0, a, :],
+            in0=freq[:],
+            scalar1=position[:, a : a + 1],
+            scalar2=1.0 / (2.0 * math.pi),
+            op0=ALU.mult,
+            op1=ALU.mult,
+        )
+    nc.vector.tensor_scalar(
+        out=turns[:, 1], in0=turns[:, 0], scalar1=0.25, scalar2=None, op0=ALU.add
+    )
+    whole = const.tile([P, 2, SEQ_TILES, N_FREQ], F32)
+    nc.vector.tensor_scalar(
+        out=whole[:],
+        in0=turns[:],
+        scalar1=ROUND_MAGIC,
+        scalar2=ROUND_MAGIC,
+        op0=ALU.add,
+        op1=ALU.subtract,
+    )
+    part = const.tile([P, 2, SEQ_TILES, N_FREQ], F32)
+    nc.vector.tensor_tensor(out=part[:], in0=turns[:], in1=whole[:], op=ALU.subtract)
+    trig = const.tile([P, 2, SEQ_TILES, N_FREQ], F32)
+    nc.scalar.activation(out=trig[:], in_=part[:], func=ACT.Sin, scale=2.0 * math.pi)
+
+    sin_pairs = trig[:, 0].rearrange("p a (i e) -> p a i e", e=2)
+    neg_sin_even = const.tile([P, SEQ_TILES, N_FREQ // 2], F32)
+    nc.vector.tensor_scalar(
+        out=neg_sin_even[:], in0=sin_pairs[:, :, :, 0], scalar1=-1.0, scalar2=None, op0=ALU.mult
+    )
+    sin_odd = const.tile([P, SEQ_TILES, N_FREQ // 2], F32)
+    nc.vector.tensor_copy(out=sin_odd[:], in_=sin_pairs[:, :, :, 1])
+    return trig[:, 1], neg_sin_even, sin_odd
+
+
+def tile_multiheadlatentattention_pa_kernel(tc, x, Wqa, q_a_norm_w, Wqb, out):
+    nc = tc.nc
+    x_rows = x.flatten_outer_dims()
+
+    with ExitStack() as ctx:
+        const = ctx.enter_context(tc.tile_pool(name="const", bufs=1))
+        keep = ctx.enter_context(tc.tile_pool(name="keep", bufs=1))
+        raw_pool = ctx.enter_context(tc.tile_pool(name="raw", bufs=4))
+        grouped_pool = ctx.enter_context(tc.tile_pool(name="grouped", bufs=4))
+        norm_pool = ctx.enter_context(tc.tile_pool(name="norm", bufs=2))
+        x_pool = ctx.enter_context(tc.tile_pool(name="x", bufs=2))
+        psum_acc = ctx.enter_context(tc.psum_pool(name="psum_acc", bufs=6))
+        psum_aux = ctx.enter_context(tc.psum_pool(name="psum_aux", bufs=2))
+
+        x_codes = keep.tile([P, TOK_TILES, X_PASSES * P], U32, align_bytes=64)
+        x_scales = keep.tile([P, TOK_TILES, X_PASSES * P], U8, align_bytes=64)
+        wqa_codes = keep.tile([P, X_PASSES, RANK], U32, align_bytes=64)
+        wqa_scales = keep.tile([P, X_PASSES, RANK], U8, align_bytes=64)
+        h_codes = keep.tile([P, TOK_TILES, H_PASSES, P], U32, align_bytes=64)
+        h_scales = keep.tile([P, TOK_TILES, H_PASSES, P], U8, align_bytes=64)
+        rope_cols = GROUP_HEADS * D_ROPE
+        nope_cols = GROUP_HEADS * D_NOPE
+        rope_codes = keep.tile([P, GROUPS, H_PASSES, rope_cols], U32, align_bytes=64)
+        rope_scales = keep.tile([P, GROUPS, H_PASSES, rope_cols], U8, align_bytes=64)
+        nope_codes = keep.tile([P, GROUPS, H_PASSES, nope_cols], U32, align_bytes=64)
+        nope_scales = keep.tile([P, GROUPS, H_PASSES, nope_cols], U8, align_bytes=64)
+
+        ident_f32 = const.tile([P, P], F32)
+        make_identity(nc, ident_f32[:])
+        ident_bf16 = const.tile([P, P], BF16)
+        make_identity(nc, ident_bf16[:])
+        cos_table, neg_sin_even, sin_odd = build_rope_tables(nc, const)
+
+        def load_and_quantise_x(i):
+            x_sb = x_pool.tile([P, D_MODEL], BF16)
+            nc.sync.dma_start(out=x_sb[:], in_=x_rows[i * P : (i + 1) * P, :])
+            x_words = x_sb[:].bitcast(F32)
+            x_grouped = x_pool.tile([P, D_MODEL], BF16, align_bytes=64)
+            x_grouped_words = x_grouped[:].bitcast(F32).rearrange(
+                "p (g r u) -> p g r u", g=X_PASSES, u=2
+            )
+            for half in range(2):
+                x_t = psum_aux.tile([P, 2, 2, P], F32, tag="aux")
+                for gg in range(2):
+                    for u in range(2):
+                        first = ((2 * half + gg) * 2 + u) * P
+                        nc.tensor.transpose(
+                            x_t[:, gg, u, :], x_words[:, first : first + P], ident_f32[:]
+                        )
+                nc.scalar.copy(
+                    out=x_grouped_words[:, 2 * half : 2 * half + 2],
+                    in_=x_t[:].rearrange("p g u r -> p g r u"),
+                )
+            nc.vector.quantize_mx(
+                out=x_codes[:, i, :].bitcast(FP8X4), scales=x_scales[:, i, :], in_=x_grouped[:]
+            )
+
+        rope_pool = ctx.enter_context(tc.tile_pool(name="rope", bufs=3))
+
+        def first_matmul(c_banks, i, g):
+            for n in range(RANK_BANKS):
+                nc.tensor.matmul_mx(
+                    out=c_banks[n][:],
+                    lhsT=x_codes[:, i, g * P : (g + 1) * P].bitcast(FP8X4),
+                    lhsT_scale=x_scales[:, i, g * P : (g + 1) * P],
+                    rhs=wqa_codes[:, g, n * BANK : (n + 1) * BANK].bitcast(FP8X4),
+                    rhs_scale=wqa_scales[:, g, n * BANK : (n + 1) * BANK],
+                    start=(g == 0),
+                    stop=(g == X_PASSES - 1),
+                )
+
+        def new_c_banks(i):
+            return [
+                psum_acc.tile([P, BANK], F32, tag="acc", name="c_%d_%d" % (i, n))
+                for n in range(RANK_BANKS)
+            ]
+
+        def norm_and_quantise(c_banks, i):
+            sum_sq = norm_pool.tile([P, RANK_BANKS], F32)
+            for n in range(RANK_BANKS):
+                squares = norm_pool.tile([P, BANK], BF16)
+                nc.scalar.activation(
+                    out=squares[:],
+                    in_=c_banks[n][:],
+                    func=ACT.Square,
+                    accum_out=sum_sq[:, n : n + 1],
+                )
+            rstd = norm_pool.tile([P, 1], F32)
+            nc.vector.tensor_reduce(
+                out=rstd[:], in_=sum_sq[:], axis=mybir.AxisListType.X, op=ALU.add
+            )
+            nc.vector.tensor_scalar(
+                out=rstd[:], in0=rstd[:], scalar1=1.0 / RANK, scalar2=EPS, op0=ALU.mult, op1=ALU.add
+            )
+            nc.scalar.sqrt(out=rstd[:], in_=rstd[:])
+            nc.vector.reciprocal(out=rstd[:], in_=rstd[:])
+
+            h_sb = norm_pool.tile([P, RANK], BF16)
+            for n in range(RANK_BANKS):
+                cols = slice(n * BANK, (n + 1) * BANK)
+                nc.vector.scalar_tensor_tensor(
+                    out=h_sb[:, cols],
+                    in0=c_banks[n][:],
+                    scalar=rstd[:, 0:1],
+                    in1=gain[:, cols],
+                    op0=ALU.mult,
+                    op1=ALU.mult,
+                )
+            for g in range(H_PASSES):
+                h_t = psum_aux.tile([P, PACK, P], BF16, tag="aux")
+                for t in range(PACK):
+                    first = g * K_PASS + t * P
+                    nc.tensor.transpose(h_t[:, t, :], h_sb[:, first : first + P], ident_bf16[:])
+                h_grouped = norm_pool.tile([P, P, PACK], BF16, align_bytes=64)
+                nc.scalar.copy(out=h_grouped[:], in_=h_t[:].rearrange("p t r -> p r t"))
+                nc.vector.quantize_mx(
+                    out=h_codes[:, i, g, :].bitcast(FP8X4),
+                    scales=h_scales[:, i, g, :],
+                    in_=h_grouped[:].rearrange("p r t -> p (r t)"),
+                )
+
+        def quantise_weights(grouped, codes, scales):
+            nc.vector.quantize_mx(
+                out=codes.bitcast(FP8X4), scales=scales, in_=grouped.rearrange("p c t -> p (c t)")
+            )
+
+        for i in range(2):
+            load_and_quantise_x(i)
+        first_pair = [new_c_banks(i) for i in range(2)]
+        for g in range(X_PASSES):
+            raw = raw_pool.tile([P, PACK, LOAD_COLS], BF16, tag="raw")
+            nc.sync.dma_start(
+                out=raw[:].rearrange("p (u e) c -> p u e c", e=2),
+                in_=Wqa[g * K_PASS : (g + 1) * K_PASS, :].rearrange(
+                    "(u q e) c -> q u e c", u=2, e=2
+                ),
+            )
+            blocks = []
+            for n in range(RANK_BANKS):
+                on_vector = (g * RANK_BANKS + n) % 2 == 1
+                grouped = grouped_pool.tile(
+                    [P, BANK, PACK],
+                    BF16,
+                    tag="by_vector" if on_vector else "by_scalar",
+                    name="wqa_grouped",
+                    align_bytes=64,
+                )
+                regroup(
+                    nc.vector.tensor_copy if on_vector else nc.scalar.copy,
+                    grouped[:],
+                    raw[:, :, n * BANK : (n + 1) * BANK].unsqueeze(2),
+                )
+                blocks.append(grouped)
+            for n in range(RANK_BANKS):
+                cols = slice(n * BANK, (n + 1) * BANK)
+                quantise_weights(blocks[n][:], wqa_codes[:, g, cols], wqa_scales[:, g, cols])
+            for i in range(2):
+                first_matmul(first_pair[i], i, g)
+        for i in range(2, TOK_TILES):
+            load_and_quantise_x(i)
+
+        gain = const.tile([P, RANK], BF16)
+        nc.sync.dma_start(out=gain[:], in_=q_a_norm_w.partition_broadcast(P))
+
+        for i in range(2):
+            norm_and_quantise(first_pair[i], i)
+        for i in range(2, TOK_TILES):
+            c_banks = new_c_banks(i)
+            for g in range(X_PASSES):
+                first_matmul(c_banks, i, g)
+            norm_and_quantise(c_banks, i)
+
+        def load_wqb(load, g):
+            raw = raw_pool.tile([P, PACK, LOAD_COLS], BF16, tag="raw")
+            nc.sync.dma_start(
+                out=raw[:],
+                in_=Wqb[
+                    g * K_PASS : (g + 1) * K_PASS, load * LOAD_COLS : (load + 1) * LOAD_COLS
+                ].rearrange("(t p) c -> p t c", p=P),
+            )
+            return raw
+
+        def quantise_group(r, raws):
+            first_head = (r % 2) * GROUP_HEADS
+            for g in range(H_PASSES):
+                four = raws[g][:].rearrange("p t (h f) -> p t h f", f=D_HEAD)[
+                    :, :, first_head : first_head + GROUP_HEADS, :
+                ]
+                rope_grouped = grouped_pool.tile(
+                    [P, rope_cols, PACK], BF16, tag="by_scalar", align_bytes=64
+                )
+                regroup(nc.scalar.copy, rope_grouped[:], four[:, :, :, D_NOPE:D_HEAD])
+                nope_grouped = grouped_pool.tile(
+                    [P, nope_cols, PACK], BF16, tag="by_vector", align_bytes=64
+                )
+                regroup(nc.vector.tensor_copy, nope_grouped[:], four[:, :, :, 0:D_NOPE])
+                quantise_weights(rope_grouped[:], rope_codes[:, r, g, :], rope_scales[:, r, g, :])
+                quantise_weights(nope_grouped[:], nope_codes[:, r, g, :], nope_scales[:, r, g, :])
+
+        def second_matmul_and_rope(r, i):
+            rope_q = psum_acc.tile([P, rope_cols], F32, tag="acc")
+            nope_q = psum_aux.tile([P, nope_cols], F32, tag="aux")
+            for g in range(H_PASSES):
+                for q_bank, codes, scales in (
+                    (rope_q, rope_codes, rope_scales),
+                    (nope_q, nope_codes, nope_scales),
+                ):
+                    nc.tensor.matmul_mx(
+                        out=q_bank[:],
+                        lhsT=h_codes[:, i, g, :].bitcast(FP8X4),
+                        lhsT_scale=h_scales[:, i, g, :],
+                        rhs=codes[:, r, g, :].bitcast(FP8X4),
+                        rhs_scale=scales[:, r, g, :],
+                        start=(g == 0),
+                        stop=(g == H_PASSES - 1),
+                    )
+
+            a = i % SEQ_TILES
+            result = rope_pool.tile([P, GROUP_HEADS, D_HEAD], F32)
+            nc.scalar.copy(
+                out=result[:, :, 0:D_NOPE], in_=nope_q[:].rearrange("p (h f) -> p h f", f=D_NOPE)
+            )
+            repeats = rope_cols // N_FREQ
+            straight = rope_pool.tile([P, rope_cols], F32)
+            nc.vector.tensor_tensor(
+                out=straight[:].rearrange("p (m j) -> p m j", j=N_FREQ),
+                in0=rope_q[:].rearrange("p (m j) -> p m j", j=N_FREQ),
+                in1=cos_table[:, a, :].unsqueeze(1).to_broadcast([P, repeats, N_FREQ]),
+                op=ALU.mult,
+            )
+            crossed = rope_pool.tile([P, 2, rope_cols // 2], F32)
+            pairs = rope_q[:].rearrange("p (m i e) -> p m i e", i=N_FREQ // 2, e=2)
+            for e, table in ((0, neg_sin_even), (1, sin_odd)):
+                nc.vector.tensor_tensor(
+                    out=crossed[:, e, :].rearrange("p (m i) -> p m i", i=N_FREQ // 2),
+                    in0=pairs[:, :, :, 1 - e],
+                    in1=table[:, a, :].unsqueeze(1).to_broadcast([P, repeats, N_FREQ // 2]),
+                    op=ALU.mult,
+                )
+            nc.vector.tensor_tensor(
+                out=result[:, :, D_NOPE:D_HEAD].rearrange("p h (i e) -> p h i e", e=2),
+                in0=straight[:].rearrange("p (h i e) -> p h i e", h=GROUP_HEADS, e=2),
+                in1=crossed[:].rearrange("p e (h i) -> p h i e", h=GROUP_HEADS),
+                op=ALU.add,
+            )
+            nc.sync.dma_start(
+                out=out[
+                    i // SEQ_TILES, r * GROUP_HEADS : (r + 1) * GROUP_HEADS, a * P : (a + 1) * P, :
+                ].rearrange("h s f -> s h f"),
+                in_=result[:],
+            )
+
+        raws = [load_wqb(0, g) for g in range(H_PASSES)]
+        quantise_group(0, raws)
+        for r in range(GROUPS):
+            if r + 1 < GROUPS:
+                if (r + 1) % 2 == 0:
+                    raws = [load_wqb((r + 1) // 2, g) for g in range(H_PASSES)]
+                quantise_group(r + 1, raws)
+            for i in range(TOK_TILES):
+                second_matmul_and_rope(r, i)

@@ -31,7 +31,9 @@ H_PASSES = RANK // K_PASS
 RANK_BANKS = RANK // BANK
 GROUP_HEADS = 4
 GROUPS = HEADS // GROUP_HEADS
-LOAD_COLS = 1536
+GROUP_COLS = GROUP_HEADS * D_HEAD
+ROPE_COLS = GROUP_HEADS * D_ROPE
+NOPE_COLS = GROUP_HEADS * D_NOPE
 ROUND_MAGIC = 12582912.0
 
 FLOPS = 2 * BATCH * SEQ * (D_MODEL * RANK + RANK * HEADS * D_HEAD)
@@ -88,6 +90,8 @@ def build_rope_tables(nc, const):
     nc.vector.tensor_tensor(out=part[:], in0=turns[:], in1=whole[:], op=ALU.subtract)
     trig = const.tile([P, 2, SEQ_TILES, N_FREQ], F32)
     nc.scalar.activation(out=trig[:], in_=part[:], func=ACT.Sin, scale=2.0 * math.pi)
+    warm = const.tile([P, 1], F32)
+    nc.scalar.sqrt(out=warm[:], in_=freq[:, 0:1])
 
     sin_pairs = trig[:, 0].rearrange("p a (i e) -> p a i e", e=2)
     neg_sin_even = const.tile([P, SEQ_TILES, N_FREQ // 2], F32)
@@ -104,14 +108,12 @@ def tile_multiheadlatentattention_pa_kernel(tc, x, Wqa, q_a_norm_w, Wqb, out):
     x_rows = x.flatten_outer_dims()
 
     with ExitStack() as ctx:
+        ctx.enter_context(tc.manual_schedule())
         const = ctx.enter_context(tc.tile_pool(name="const", bufs=1))
         keep = ctx.enter_context(tc.tile_pool(name="keep", bufs=1))
-        raw_pool = ctx.enter_context(tc.tile_pool(name="raw", bufs=4))
         grouped_pool = ctx.enter_context(tc.tile_pool(name="grouped", bufs=4))
         norm_pool = ctx.enter_context(tc.tile_pool(name="norm", bufs=2))
-        x_pool = ctx.enter_context(tc.tile_pool(name="x", bufs=2))
-        psum_acc = ctx.enter_context(tc.psum_pool(name="psum_acc", bufs=6))
-        psum_aux = ctx.enter_context(tc.psum_pool(name="psum_aux", bufs=2))
+        psum = ctx.enter_context(tc.psum_pool(name="psum", bufs=8))
 
         x_codes = keep.tile([P, TOK_TILES, X_PASSES * P], U32, align_bytes=64)
         x_scales = keep.tile([P, TOK_TILES, X_PASSES * P], U8, align_bytes=64)
@@ -119,44 +121,28 @@ def tile_multiheadlatentattention_pa_kernel(tc, x, Wqa, q_a_norm_w, Wqb, out):
         wqa_scales = keep.tile([P, X_PASSES, RANK], U8, align_bytes=64)
         h_codes = keep.tile([P, TOK_TILES, H_PASSES, P], U32, align_bytes=64)
         h_scales = keep.tile([P, TOK_TILES, H_PASSES, P], U8, align_bytes=64)
-        rope_cols = GROUP_HEADS * D_ROPE
-        nope_cols = GROUP_HEADS * D_NOPE
-        rope_codes = keep.tile([P, GROUPS, H_PASSES, rope_cols], U32, align_bytes=64)
-        rope_scales = keep.tile([P, GROUPS, H_PASSES, rope_cols], U8, align_bytes=64)
-        nope_codes = keep.tile([P, GROUPS, H_PASSES, nope_cols], U32, align_bytes=64)
-        nope_scales = keep.tile([P, GROUPS, H_PASSES, nope_cols], U8, align_bytes=64)
+        rope_codes = keep.tile([P, GROUPS, H_PASSES, ROPE_COLS], U32, align_bytes=64)
+        rope_scales = keep.tile([P, GROUPS, H_PASSES, ROPE_COLS], U8, align_bytes=64)
+        nope_codes = keep.tile([P, GROUPS, H_PASSES, NOPE_COLS], U32, align_bytes=64)
+        nope_scales = keep.tile([P, GROUPS, H_PASSES, NOPE_COLS], U8, align_bytes=64)
 
         ident_f32 = const.tile([P, P], F32)
         make_identity(nc, ident_f32[:])
         ident_bf16 = const.tile([P, P], BF16)
         make_identity(nc, ident_bf16[:])
         cos_table, neg_sin_even, sin_odd = build_rope_tables(nc, const)
+        gain = const.tile([P, RANK], BF16)
 
-        def load_and_quantise_x(i):
-            x_sb = x_pool.tile([P, D_MODEL], BF16)
-            nc.sync.dma_start(out=x_sb[:], in_=x_rows[i * P : (i + 1) * P, :])
-            x_words = x_sb[:].bitcast(F32)
-            x_grouped = x_pool.tile([P, D_MODEL], BF16, align_bytes=64)
-            x_grouped_words = x_grouped[:].bitcast(F32).rearrange(
-                "p (g r u) -> p g r u", g=X_PASSES, u=2
-            )
-            for half in range(2):
-                x_t = psum_aux.tile([P, 2, 2, P], F32, tag="aux")
-                for gg in range(2):
-                    for u in range(2):
-                        first = ((2 * half + gg) * 2 + u) * P
-                        nc.tensor.transpose(
-                            x_t[:, gg, u, :], x_words[:, first : first + P], ident_f32[:]
-                        )
-                nc.scalar.copy(
-                    out=x_grouped_words[:, 2 * half : 2 * half + 2],
-                    in_=x_t[:].rearrange("p g u r -> p g r u"),
-                )
+        def quantise(grouped, codes, scales):
             nc.vector.quantize_mx(
-                out=x_codes[:, i, :].bitcast(FP8X4), scales=x_scales[:, i, :], in_=x_grouped[:]
+                out=codes.bitcast(FP8X4), scales=scales, in_=grouped.rearrange("p c t -> p (c t)")
             )
 
-        rope_pool = ctx.enter_context(tc.tile_pool(name="rope", bufs=3))
+        def new_c_banks(i):
+            return [
+                psum.tile([P, BANK], F32, tag="bank", name="c_%d_%d" % (i, n))
+                for n in range(RANK_BANKS)
+            ]
 
         def first_matmul(c_banks, i, g):
             for n in range(RANK_BANKS):
@@ -170,137 +156,208 @@ def tile_multiheadlatentattention_pa_kernel(tc, x, Wqa, q_a_norm_w, Wqb, out):
                     stop=(g == X_PASSES - 1),
                 )
 
-        def new_c_banks(i):
-            return [
-                psum_acc.tile([P, BANK], F32, tag="acc", name="c_%d_%d" % (i, n))
-                for n in range(RANK_BANKS)
-            ]
-
-        def norm_and_quantise(c_banks, i):
-            sum_sq = norm_pool.tile([P, RANK_BANKS], F32)
-            for n in range(RANK_BANKS):
-                squares = norm_pool.tile([P, BANK], BF16)
-                nc.scalar.activation(
-                    out=squares[:],
-                    in_=c_banks[n][:],
-                    func=ACT.Square,
-                    accum_out=sum_sq[:, n : n + 1],
+        c_banks = {}
+        with tc.tile_pool(name="x", bufs=TOK_TILES) as x_pool, tc.tile_pool(
+            name="wqa_raw", bufs=X_PASSES
+        ) as wqa_pool:
+            x_tiles = []
+            for i in range(TOK_TILES):
+                x_sb = x_pool.tile([P, D_MODEL], BF16)
+                nc.sync.dma_start(out=x_sb[:], in_=x_rows[i * P : (i + 1) * P, :])
+                x_tiles.append(x_sb)
+            wqa_tiles = []
+            for g in range(X_PASSES):
+                wqa_raw = wqa_pool.tile([P, PACK, RANK], BF16)
+                nc.sync.dma_start(
+                    out=wqa_raw[:].rearrange("p (u e) c -> p u e c", e=2),
+                    in_=Wqa[g * K_PASS : (g + 1) * K_PASS, :].rearrange(
+                        "(u q e) c -> q u e c", u=2, e=2
+                    ),
                 )
-            rstd = norm_pool.tile([P, 1], F32)
+                wqa_tiles.append(wqa_raw)
+            nc.sync.dma_start(out=gain[:], in_=q_a_norm_w.partition_broadcast(P))
+
+            for i in range(TOK_TILES):
+                x_words = x_tiles[i][:].bitcast(F32)
+                x_grouped = x_pool.tile([P, D_MODEL], BF16, bufs=2, align_bytes=64)
+                x_grouped_words = x_grouped[:].bitcast(F32).rearrange(
+                    "p (g r u) -> p g r u", g=X_PASSES, u=2
+                )
+                for half in range(2):
+                    x_t = psum.tile([P, 2, 2, P], F32, tag="bank")
+                    for gg in range(2):
+                        for u in range(2):
+                            first = ((2 * half + gg) * 2 + u) * P
+                            nc.tensor.transpose(
+                                x_t[:, gg, u, :], x_words[:, first : first + P], ident_f32[:]
+                            )
+                    nc.scalar.copy(
+                        out=x_grouped_words[:, 2 * half : 2 * half + 2],
+                        in_=x_t[:].rearrange("p g u r -> p g r u"),
+                    )
+                nc.vector.quantize_mx(
+                    out=x_codes[:, i, :].bitcast(FP8X4), scales=x_scales[:, i, :], in_=x_grouped[:]
+                )
+
+            for i in range(2):
+                c_banks[i] = new_c_banks(i)
+            for g in range(X_PASSES):
+                blocks = []
+                for n in range(RANK_BANKS):
+                    on_vector = (g * RANK_BANKS + n) % 2 == 1
+                    wqa_grouped = grouped_pool.tile(
+                        [P, BANK, PACK], BF16, tag="grouped_512", align_bytes=64
+                    )
+                    regroup(
+                        nc.vector.tensor_copy if on_vector else nc.scalar.copy,
+                        wqa_grouped[:],
+                        wqa_tiles[g][:, :, n * BANK : (n + 1) * BANK].unsqueeze(2),
+                    )
+                    blocks.append(wqa_grouped)
+                for n in range(RANK_BANKS):
+                    cols = slice(n * BANK, (n + 1) * BANK)
+                    quantise(blocks[n][:], wqa_codes[:, g, cols], wqa_scales[:, g, cols])
+                for i in range(2):
+                    first_matmul(c_banks[i], i, g)
+
+        wqb_pool = ctx.enter_context(tc.tile_pool(name="wqb_raw", bufs=8, reuse_waits="tile"))
+        rope_pool = ctx.enter_context(tc.tile_pool(name="rope", bufs=3, reuse_waits="tile"))
+
+        wqb_tiles = {}
+        for r in range(GROUPS):
+            for g in range(H_PASSES):
+                wqb_raw = wqb_pool.tile([P, PACK, GROUP_COLS], BF16)
+                nc.sync.dma_start(
+                    out=wqb_raw[:],
+                    in_=Wqb[
+                        g * K_PASS : (g + 1) * K_PASS, r * GROUP_COLS : (r + 1) * GROUP_COLS
+                    ].rearrange("(t p) c -> p t c", p=P),
+                )
+                wqb_tiles[(r, g)] = wqb_raw
+
+        wqb_grouped = {}
+
+        def regroup_wqb(r, g):
+            copy = nc.vector.tensor_copy if r == 0 else nc.scalar.copy
+            by_head = wqb_tiles[(r, g)][:].rearrange("p t (h f) -> p t h f", f=D_HEAD)
+            rope_grouped = grouped_pool.tile(
+                [P, ROPE_COLS, PACK], BF16, tag="grouped_512", align_bytes=64
+            )
+            regroup(copy, rope_grouped[:], by_head[:, :, :, D_NOPE:D_HEAD])
+            nope_grouped = grouped_pool.tile(
+                [P, NOPE_COLS, PACK], BF16, tag="grouped_256", align_bytes=64
+            )
+            regroup(copy, nope_grouped[:], by_head[:, :, :, 0:D_NOPE])
+            wqb_grouped[(r, g)] = (rope_grouped, nope_grouped)
+
+        def quantise_wqb(r, g):
+            rope_grouped, nope_grouped = wqb_grouped[(r, g)]
+            quantise(rope_grouped[:], rope_codes[:, r, g, :], rope_scales[:, r, g, :])
+            quantise(nope_grouped[:], nope_codes[:, r, g, :], nope_scales[:, r, g, :])
+
+        sum_sq = {}
+        rstd = {}
+        h_rows = {}
+        h_grouped = {}
+
+        def square(i, n):
+            if n == 0:
+                sum_sq[i] = norm_pool.tile([P, RANK_BANKS], F32, name="sum_sq")
+            squares = norm_pool.tile([P, BANK], BF16)
+            nc.scalar.activation(
+                out=squares[:],
+                in_=c_banks[i][n][:],
+                func=ACT.Square,
+                accum_out=sum_sq[i][:, n : n + 1],
+            )
+
+        def mean_square(i):
+            rstd[i] = norm_pool.tile([P, 1], F32, name="rstd")
             nc.vector.tensor_reduce(
-                out=rstd[:], in_=sum_sq[:], axis=mybir.AxisListType.X, op=ALU.add
+                out=rstd[i][:], in_=sum_sq[i][:], axis=mybir.AxisListType.X, op=ALU.add
             )
             nc.vector.tensor_scalar(
-                out=rstd[:], in0=rstd[:], scalar1=1.0 / RANK, scalar2=EPS, op0=ALU.mult, op1=ALU.add
+                out=rstd[i][:],
+                in0=rstd[i][:],
+                scalar1=1.0 / RANK,
+                scalar2=EPS,
+                op0=ALU.mult,
+                op1=ALU.add,
             )
-            nc.scalar.sqrt(out=rstd[:], in_=rstd[:])
-            nc.vector.reciprocal(out=rstd[:], in_=rstd[:])
 
-            h_sb = norm_pool.tile([P, RANK], BF16)
+        def scale_and_transpose(i, n):
+            if n == 0:
+                h_rows[i] = norm_pool.tile([P, RANK], BF16, name="h_rows")
+            cols = slice(n * BANK, (n + 1) * BANK)
+            nc.vector.scalar_tensor_tensor(
+                out=h_rows[i][:, cols],
+                in0=c_banks[i][n][:],
+                scalar=rstd[i][:, 0:1],
+                in1=gain[:, cols],
+                op0=ALU.mult,
+                op1=ALU.mult,
+            )
+            h_t = psum.tile([P, PACK, P], BF16, tag="bank")
+            for t in range(PACK):
+                first = n * K_PASS + t * P
+                nc.tensor.transpose(h_t[:, t, :], h_rows[i][:, first : first + P], ident_bf16[:])
+            h_grouped[(i, n)] = h_t
+
+        def copy_h(i, g):
+            h_t = h_grouped[(i, g)]
+            h_words = norm_pool.tile([P, P, PACK], BF16, bufs=6, align_bytes=64)
+            nc.scalar.copy(out=h_words[:], in_=h_t[:].rearrange("p t r -> p r t"))
+            h_grouped[(i, g)] = h_words
+
+        def quantise_h(i, g):
+            quantise(h_grouped[(i, g)][:], h_codes[:, i, g, :], h_scales[:, i, g, :])
+
+        def norm_two_tiles(i0, i1):
             for n in range(RANK_BANKS):
-                cols = slice(n * BANK, (n + 1) * BANK)
-                nc.vector.scalar_tensor_tensor(
-                    out=h_sb[:, cols],
-                    in0=c_banks[n][:],
-                    scalar=rstd[:, 0:1],
-                    in1=gain[:, cols],
-                    op0=ALU.mult,
-                    op1=ALU.mult,
-                )
+                square(i0, n)
+            mean_square(i0)
+            square(i1, 0)
+            nc.scalar.sqrt(out=rstd[i0][:], in_=rstd[i0][:])
+            nc.vector.reciprocal(out=rstd[i0][:], in_=rstd[i0][:])
+            square(i1, 1)
+            square(i1, 2)
+            scale_and_transpose(i0, 0)
+            scale_and_transpose(i0, 1)
+            mean_square(i1)
+            nc.scalar.sqrt(out=rstd[i1][:], in_=rstd[i1][:])
+            scale_and_transpose(i0, 2)
+            nc.vector.reciprocal(out=rstd[i1][:], in_=rstd[i1][:])
             for g in range(H_PASSES):
-                h_t = psum_aux.tile([P, PACK, P], BF16, tag="aux")
-                for t in range(PACK):
-                    first = g * K_PASS + t * P
-                    nc.tensor.transpose(h_t[:, t, :], h_sb[:, first : first + P], ident_bf16[:])
-                h_grouped = norm_pool.tile([P, P, PACK], BF16, align_bytes=64)
-                nc.scalar.copy(out=h_grouped[:], in_=h_t[:].rearrange("p t r -> p r t"))
-                nc.vector.quantize_mx(
-                    out=h_codes[:, i, g, :].bitcast(FP8X4),
-                    scales=h_scales[:, i, g, :],
-                    in_=h_grouped[:].rearrange("p r t -> p (r t)"),
-                )
-
-        def quantise_weights(grouped, codes, scales):
-            nc.vector.quantize_mx(
-                out=codes.bitcast(FP8X4), scales=scales, in_=grouped.rearrange("p c t -> p (c t)")
-            )
-
-        for i in range(2):
-            load_and_quantise_x(i)
-        first_pair = [new_c_banks(i) for i in range(2)]
-        for g in range(X_PASSES):
-            raw = raw_pool.tile([P, PACK, LOAD_COLS], BF16, tag="raw")
-            nc.sync.dma_start(
-                out=raw[:].rearrange("p (u e) c -> p u e c", e=2),
-                in_=Wqa[g * K_PASS : (g + 1) * K_PASS, :].rearrange(
-                    "(u q e) c -> q u e c", u=2, e=2
-                ),
-            )
-            blocks = []
+                copy_h(i0, g)
             for n in range(RANK_BANKS):
-                on_vector = (g * RANK_BANKS + n) % 2 == 1
-                grouped = grouped_pool.tile(
-                    [P, BANK, PACK],
-                    BF16,
-                    tag="by_vector" if on_vector else "by_scalar",
-                    name="wqa_grouped",
-                    align_bytes=64,
-                )
-                regroup(
-                    nc.vector.tensor_copy if on_vector else nc.scalar.copy,
-                    grouped[:],
-                    raw[:, :, n * BANK : (n + 1) * BANK].unsqueeze(2),
-                )
-                blocks.append(grouped)
-            for n in range(RANK_BANKS):
-                cols = slice(n * BANK, (n + 1) * BANK)
-                quantise_weights(blocks[n][:], wqa_codes[:, g, cols], wqa_scales[:, g, cols])
-            for i in range(2):
-                first_matmul(first_pair[i], i, g)
-        for i in range(2, TOK_TILES):
-            load_and_quantise_x(i)
+                scale_and_transpose(i1, n)
 
-        gain = const.tile([P, RANK], BF16)
-        nc.sync.dma_start(out=gain[:], in_=q_a_norm_w.partition_broadcast(P))
+        def finish_two_tiles(i0, i1):
+            for g in range(H_PASSES):
+                quantise_h(i0, g)
+            for g in range(H_PASSES):
+                copy_h(i1, g)
+            for g in range(H_PASSES):
+                quantise_h(i1, g)
 
-        for i in range(2):
-            norm_and_quantise(first_pair[i], i)
+        norm_two_tiles(0, 1)
         for i in range(2, TOK_TILES):
-            c_banks = new_c_banks(i)
+            c_banks[i] = new_c_banks(i)
             for g in range(X_PASSES):
-                first_matmul(c_banks, i, g)
-            norm_and_quantise(c_banks, i)
-
-        def load_wqb(load, g):
-            raw = raw_pool.tile([P, PACK, LOAD_COLS], BF16, tag="raw")
-            nc.sync.dma_start(
-                out=raw[:],
-                in_=Wqb[
-                    g * K_PASS : (g + 1) * K_PASS, load * LOAD_COLS : (load + 1) * LOAD_COLS
-                ].rearrange("(t p) c -> p t c", p=P),
-            )
-            return raw
-
-        def quantise_group(r, raws):
-            first_head = (r % 2) * GROUP_HEADS
-            for g in range(H_PASSES):
-                four = raws[g][:].rearrange("p t (h f) -> p t h f", f=D_HEAD)[
-                    :, :, first_head : first_head + GROUP_HEADS, :
-                ]
-                rope_grouped = grouped_pool.tile(
-                    [P, rope_cols, PACK], BF16, tag="by_scalar", align_bytes=64
-                )
-                regroup(nc.scalar.copy, rope_grouped[:], four[:, :, :, D_NOPE:D_HEAD])
-                nope_grouped = grouped_pool.tile(
-                    [P, nope_cols, PACK], BF16, tag="by_vector", align_bytes=64
-                )
-                regroup(nc.vector.tensor_copy, nope_grouped[:], four[:, :, :, 0:D_NOPE])
-                quantise_weights(rope_grouped[:], rope_codes[:, r, g, :], rope_scales[:, r, g, :])
-                quantise_weights(nope_grouped[:], nope_codes[:, r, g, :], nope_scales[:, r, g, :])
+                first_matmul(c_banks[i], i, g)
+        finish_two_tiles(0, 1)
+        regroup_wqb(0, 0)
+        regroup_wqb(0, 1)
+        quantise_wqb(0, 0)
+        norm_two_tiles(2, 3)
+        finish_two_tiles(2, 3)
+        regroup_wqb(0, 2)
+        quantise_wqb(0, 1)
+        quantise_wqb(0, 2)
 
         def second_matmul_and_rope(r, i):
-            rope_q = psum_acc.tile([P, rope_cols], F32, tag="acc")
-            nope_q = psum_aux.tile([P, nope_cols], F32, tag="aux")
+            rope_q = psum.tile([P, ROPE_COLS], F32, tag="bank")
+            nope_q = psum.tile([P, NOPE_COLS], F32, tag="bank")
             for g in range(H_PASSES):
                 for q_bank, codes, scales in (
                     (rope_q, rope_codes, rope_scales),
@@ -317,19 +374,19 @@ def tile_multiheadlatentattention_pa_kernel(tc, x, Wqa, q_a_norm_w, Wqb, out):
                     )
 
             a = i % SEQ_TILES
-            result = rope_pool.tile([P, GROUP_HEADS, D_HEAD], F32)
+            result = rope_pool.tile([P, GROUP_HEADS, D_HEAD], F32, bufs=6)
             nc.scalar.copy(
                 out=result[:, :, 0:D_NOPE], in_=nope_q[:].rearrange("p (h f) -> p h f", f=D_NOPE)
             )
-            repeats = rope_cols // N_FREQ
-            straight = rope_pool.tile([P, rope_cols], F32)
+            repeats = ROPE_COLS // N_FREQ
+            straight = rope_pool.tile([P, ROPE_COLS], F32)
             nc.vector.tensor_tensor(
                 out=straight[:].rearrange("p (m j) -> p m j", j=N_FREQ),
                 in0=rope_q[:].rearrange("p (m j) -> p m j", j=N_FREQ),
                 in1=cos_table[:, a, :].unsqueeze(1).to_broadcast([P, repeats, N_FREQ]),
                 op=ALU.mult,
             )
-            crossed = rope_pool.tile([P, 2, rope_cols // 2], F32)
+            crossed = rope_pool.tile([P, 2, ROPE_COLS // 2], F32)
             pairs = rope_q[:].rearrange("p (m i e) -> p m i e", i=N_FREQ // 2, e=2)
             for e, table in ((0, neg_sin_even), (1, sin_odd)):
                 nc.vector.tensor_tensor(
@@ -351,12 +408,10 @@ def tile_multiheadlatentattention_pa_kernel(tc, x, Wqa, q_a_norm_w, Wqb, out):
                 in_=result[:],
             )
 
-        raws = [load_wqb(0, g) for g in range(H_PASSES)]
-        quantise_group(0, raws)
         for r in range(GROUPS):
-            if r + 1 < GROUPS:
-                if (r + 1) % 2 == 0:
-                    raws = [load_wqb((r + 1) // 2, g) for g in range(H_PASSES)]
-                quantise_group(r + 1, raws)
             for i in range(TOK_TILES):
+                if r + 1 < GROUPS and i < H_PASSES:
+                    regroup_wqb(r + 1, i)
                 second_matmul_and_rope(r, i)
+                if r + 1 < GROUPS and i > 0:
+                    quantise_wqb(r + 1, i - 1)

@@ -108,7 +108,6 @@ def tile_multiheadlatentattention_pa_kernel(tc, x, Wqa, q_a_norm_w, Wqb, out):
     x_rows = x.flatten_outer_dims()
 
     with ExitStack() as ctx:
-        ctx.enter_context(tc.manual_schedule())
         const = ctx.enter_context(tc.tile_pool(name="const", bufs=1))
         keep = ctx.enter_context(tc.tile_pool(name="keep", bufs=1))
         grouped_pool = ctx.enter_context(tc.tile_pool(name="grouped", bufs=4))
@@ -144,8 +143,8 @@ def tile_multiheadlatentattention_pa_kernel(tc, x, Wqa, q_a_norm_w, Wqb, out):
                 for n in range(RANK_BANKS)
             ]
 
-        def first_matmul(c_banks, i, g):
-            for n in range(RANK_BANKS):
+        def first_matmul(c_banks, i, g, banks):
+            for n in banks:
                 nc.tensor.matmul_mx(
                     out=c_banks[n][:],
                     lhsT=x_codes[:, i, g * P : (g + 1) * P].bitcast(FP8X4),
@@ -160,11 +159,12 @@ def tile_multiheadlatentattention_pa_kernel(tc, x, Wqa, q_a_norm_w, Wqb, out):
         with tc.tile_pool(name="x", bufs=TOK_TILES) as x_pool, tc.tile_pool(
             name="wqa_raw", bufs=X_PASSES
         ) as wqa_pool:
-            x_tiles = []
-            for i in range(TOK_TILES):
+            def load_x(i):
                 x_sb = x_pool.tile([P, D_MODEL], BF16)
                 nc.sync.dma_start(out=x_sb[:], in_=x_rows[i * P : (i + 1) * P, :])
-                x_tiles.append(x_sb)
+                return x_sb
+
+            x_tiles = [load_x(i) for i in range(2)]
             wqa_tiles = []
             for g in range(X_PASSES):
                 wqa_raw = wqa_pool.tile([P, PACK, RANK], BF16)
@@ -175,9 +175,10 @@ def tile_multiheadlatentattention_pa_kernel(tc, x, Wqa, q_a_norm_w, Wqb, out):
                     ),
                 )
                 wqa_tiles.append(wqa_raw)
+            x_tiles.extend([load_x(i) for i in range(2, TOK_TILES)])
             nc.sync.dma_start(out=gain[:], in_=q_a_norm_w.partition_broadcast(P))
 
-            for i in range(TOK_TILES):
+            def quantise_x(i):
                 x_words = x_tiles[i][:].bitcast(F32)
                 x_grouped = x_pool.tile([P, D_MODEL], BF16, bufs=2, align_bytes=64)
                 x_grouped_words = x_grouped[:].bitcast(F32).rearrange(
@@ -200,6 +201,9 @@ def tile_multiheadlatentattention_pa_kernel(tc, x, Wqa, q_a_norm_w, Wqb, out):
                 )
 
             for i in range(2):
+                quantise_x(i)
+
+            for i in range(2):
                 c_banks[i] = new_c_banks(i)
             for g in range(X_PASSES):
                 blocks = []
@@ -218,9 +222,11 @@ def tile_multiheadlatentattention_pa_kernel(tc, x, Wqa, q_a_norm_w, Wqb, out):
                     cols = slice(n * BANK, (n + 1) * BANK)
                     quantise(blocks[n][:], wqa_codes[:, g, cols], wqa_scales[:, g, cols])
                 for i in range(2):
-                    first_matmul(c_banks[i], i, g)
+                    first_matmul(c_banks[i], i, g, range(RANK_BANKS))
+            for i in range(2, TOK_TILES):
+                quantise_x(i)
 
-        wqb_pool = ctx.enter_context(tc.tile_pool(name="wqb_raw", bufs=8, reuse_waits="tile"))
+        wqb_pool = ctx.enter_context(tc.tile_pool(name="wqb_raw", bufs=6, reuse_waits="tile"))
         rope_pool = ctx.enter_context(tc.tile_pool(name="rope", bufs=3, reuse_waits="tile"))
 
         wqb_tiles = {}
@@ -238,16 +244,23 @@ def tile_multiheadlatentattention_pa_kernel(tc, x, Wqa, q_a_norm_w, Wqb, out):
         wqb_grouped = {}
 
         def regroup_wqb(r, g):
-            copy = nc.vector.tensor_copy if r == 0 else nc.scalar.copy
             by_head = wqb_tiles[(r, g)][:].rearrange("p t (h f) -> p t h f", f=D_HEAD)
             rope_grouped = grouped_pool.tile(
                 [P, ROPE_COLS, PACK], BF16, tag="grouped_512", align_bytes=64
             )
-            regroup(copy, rope_grouped[:], by_head[:, :, :, D_NOPE:D_HEAD])
+            if r < 2:
+                regroup(nc.vector.tensor_copy, rope_grouped[:], by_head[:, :, :, D_NOPE:D_HEAD])
+            else:
+                for h in range(GROUP_HEADS):
+                    regroup(
+                        nc.scalar.copy,
+                        rope_grouped[:, h * D_ROPE : (h + 1) * D_ROPE, :],
+                        by_head[:, :, h : h + 1, D_NOPE:D_HEAD],
+                    )
             nope_grouped = grouped_pool.tile(
                 [P, NOPE_COLS, PACK], BF16, tag="grouped_256", align_bytes=64
             )
-            regroup(copy, nope_grouped[:], by_head[:, :, :, 0:D_NOPE])
+            regroup(nc.scalar.copy, nope_grouped[:], by_head[:, :, :, 0:D_NOPE])
             wqb_grouped[(r, g)] = (rope_grouped, nope_grouped)
 
         def quantise_wqb(r, g):
@@ -312,48 +325,51 @@ def tile_multiheadlatentattention_pa_kernel(tc, x, Wqa, q_a_norm_w, Wqb, out):
         def quantise_h(i, g):
             quantise(h_grouped[(i, g)][:], h_codes[:, i, g, :], h_scales[:, i, g, :])
 
-        def norm_two_tiles(i0, i1):
+        def norm_front(i):
             for n in range(RANK_BANKS):
-                square(i0, n)
-            mean_square(i0)
-            square(i1, 0)
-            nc.scalar.sqrt(out=rstd[i0][:], in_=rstd[i0][:])
-            nc.vector.reciprocal(out=rstd[i0][:], in_=rstd[i0][:])
-            square(i1, 1)
-            square(i1, 2)
-            scale_and_transpose(i0, 0)
-            scale_and_transpose(i0, 1)
-            mean_square(i1)
-            nc.scalar.sqrt(out=rstd[i1][:], in_=rstd[i1][:])
-            scale_and_transpose(i0, 2)
-            nc.vector.reciprocal(out=rstd[i1][:], in_=rstd[i1][:])
-            for g in range(H_PASSES):
-                copy_h(i0, g)
+                square(i, n)
+
+        def move_c_to_sbuf(i):
+            c_rows = norm_pool.tile([P, RANK], F32)
             for n in range(RANK_BANKS):
-                scale_and_transpose(i1, n)
+                nc.vector.tensor_copy(out=c_rows[:, n * BANK : (n + 1) * BANK], in_=c_banks[i][n][:])
+            c_banks[i] = [c_rows[:, n * BANK : (n + 1) * BANK] for n in range(RANK_BANKS)]
 
-        def finish_two_tiles(i0, i1):
-            for g in range(H_PASSES):
-                quantise_h(i0, g)
-            for g in range(H_PASSES):
-                copy_h(i1, g)
-            for g in range(H_PASSES):
-                quantise_h(i1, g)
+        def norm_middle(i):
+            mean_square(i)
+            nc.scalar.sqrt(out=rstd[i][:], in_=rstd[i][:])
+            nc.vector.reciprocal(out=rstd[i][:], in_=rstd[i][:])
+            for n in range(RANK_BANKS):
+                scale_and_transpose(i, n)
 
-        norm_two_tiles(0, 1)
+        def norm_back(i):
+            for g in range(H_PASSES):
+                copy_h(i, g)
+            for g in range(H_PASSES):
+                quantise_h(i, g)
+
+        for i in range(2):
+            norm_front(i)
+            move_c_to_sbuf(i)
         for i in range(2, TOK_TILES):
             c_banks[i] = new_c_banks(i)
-            for g in range(X_PASSES):
-                first_matmul(c_banks[i], i, g)
-        finish_two_tiles(0, 1)
-        regroup_wqb(0, 0)
-        regroup_wqb(0, 1)
-        quantise_wqb(0, 0)
-        norm_two_tiles(2, 3)
-        finish_two_tiles(2, 3)
-        regroup_wqb(0, 2)
-        quantise_wqb(0, 1)
-        quantise_wqb(0, 2)
+            for n in range(RANK_BANKS):
+                for g in range(X_PASSES):
+                    first_matmul(c_banks[i], i, g, [n])
+        for i in range(2):
+            norm_middle(i)
+        for i in range(2):
+            norm_back(i)
+        for i in range(2, TOK_TILES):
+            norm_front(i)
+        for i in range(2, TOK_TILES):
+            norm_middle(i)
+        for i in range(2, TOK_TILES):
+            norm_back(i)
+        for g in range(H_PASSES):
+            regroup_wqb(0, g)
+        for g in range(H_PASSES):
+            quantise_wqb(0, g)
 
         def second_matmul_and_rope(r, i):
             rope_q = psum.tile([P, ROPE_COLS], F32, tag="bank")
@@ -379,14 +395,14 @@ def tile_multiheadlatentattention_pa_kernel(tc, x, Wqa, q_a_norm_w, Wqb, out):
                 out=result[:, :, 0:D_NOPE], in_=nope_q[:].rearrange("p (h f) -> p h f", f=D_NOPE)
             )
             repeats = ROPE_COLS // N_FREQ
-            straight = rope_pool.tile([P, ROPE_COLS], F32)
+            straight = rope_pool.tile([P, ROPE_COLS], F32, bufs=5)
             nc.vector.tensor_tensor(
                 out=straight[:].rearrange("p (m j) -> p m j", j=N_FREQ),
                 in0=rope_q[:].rearrange("p (m j) -> p m j", j=N_FREQ),
                 in1=cos_table[:, a, :].unsqueeze(1).to_broadcast([P, repeats, N_FREQ]),
                 op=ALU.mult,
             )
-            crossed = rope_pool.tile([P, 2, ROPE_COLS // 2], F32)
+            crossed = rope_pool.tile([P, 2, ROPE_COLS // 2], F32, bufs=5)
             pairs = rope_q[:].rearrange("p (m i e) -> p m i e", i=N_FREQ // 2, e=2)
             for e, table in ((0, neg_sin_even), (1, sin_odd)):
                 nc.vector.tensor_tensor(
@@ -395,7 +411,9 @@ def tile_multiheadlatentattention_pa_kernel(tc, x, Wqa, q_a_norm_w, Wqb, out):
                     in1=table[:, a, :].unsqueeze(1).to_broadcast([P, repeats, N_FREQ // 2]),
                     op=ALU.mult,
                 )
-            nc.vector.tensor_tensor(
+            last = r == GROUPS - 1 and i == TOK_TILES - 1
+            adder = nc.vector if last else nc.gpsimd
+            adder.tensor_tensor(
                 out=result[:, :, D_NOPE:D_HEAD].rearrange("p h (i e) -> p h i e", e=2),
                 in0=straight[:].rearrange("p (h i e) -> p h i e", h=GROUP_HEADS, e=2),
                 in1=crossed[:].rearrange("p e (h i) -> p h i e", h=GROUP_HEADS),

@@ -130,7 +130,20 @@ def tile_multiheadlatentattention_pa_kernel(tc, x, Wqa, q_a_norm_w, Wqb, out):
         ident_bf16 = const.tile([P, P], BF16)
         make_identity(nc, ident_bf16[:])
         cos_table, neg_sin_even, sin_odd = build_rope_tables(nc, const)
+
+        gain_row = const.tile([P, RANK], BF16)
+        nc.vector.memset(gain_row[:].bitcast(I32), 0)
+        nc.sync.dma_start(out=gain_row[0:1, :], in_=q_a_norm_w.unsqueeze(0))
+        ones = const.tile([P, P], BF16)
+        nc.vector.memset(ones[:], 1.0)
         gain = const.tile([P, RANK], BF16)
+        for n in range(RANK_BANKS):
+            cols = slice(n * BANK, (n + 1) * BANK)
+            gain_bank = psum.tile([P, BANK], F32, tag="bank")
+            nc.tensor.matmul(
+                out=gain_bank[:], lhsT=ones[:], rhs=gain_row[:, cols], start=True, stop=True
+            )
+            nc.vector.tensor_copy(out=gain[:, cols], in_=gain_bank[:])
 
         def quantise(grouped, codes, scales):
             nc.vector.quantize_mx(
@@ -176,7 +189,6 @@ def tile_multiheadlatentattention_pa_kernel(tc, x, Wqa, q_a_norm_w, Wqb, out):
                 )
                 wqa_tiles.append(wqa_raw)
             x_tiles.extend([load_x(i) for i in range(2, TOK_TILES)])
-            nc.sync.dma_start(out=gain[:], in_=q_a_norm_w.partition_broadcast(P))
 
             def quantise_x(i):
                 x_words = x_tiles[i][:].bitcast(F32)
@@ -243,13 +255,23 @@ def tile_multiheadlatentattention_pa_kernel(tc, x, Wqa, q_a_norm_w, Wqb, out):
 
         wqb_grouped = {}
 
+        def gpsimd_regroup(grouped, rows):
+            nc.gpsimd.tensor_scalar(
+                out=grouped.rearrange("p (n w) t -> p n w t", n=rows.shape[2]),
+                in0=rows.rearrange("p t n w -> p n w t"),
+                scalar1=1.0,
+                scalar2=0.0,
+                op0=ALU.mult,
+                op1=ALU.add,
+            )
+
         def regroup_wqb(r, g):
             by_head = wqb_tiles[(r, g)][:].rearrange("p t (h f) -> p t h f", f=D_HEAD)
             rope_grouped = grouped_pool.tile(
                 [P, ROPE_COLS, PACK], BF16, tag="grouped_512", align_bytes=64
             )
-            if r < 2:
-                regroup(nc.vector.tensor_copy, rope_grouped[:], by_head[:, :, :, D_NOPE:D_HEAD])
+            if r == 0:
+                gpsimd_regroup(rope_grouped[:], by_head[:, :, :, D_NOPE:D_HEAD])
             else:
                 for h in range(GROUP_HEADS):
                     regroup(
@@ -260,7 +282,7 @@ def tile_multiheadlatentattention_pa_kernel(tc, x, Wqa, q_a_norm_w, Wqb, out):
             nope_grouped = grouped_pool.tile(
                 [P, NOPE_COLS, PACK], BF16, tag="grouped_256", align_bytes=64
             )
-            regroup(nc.scalar.copy, nope_grouped[:], by_head[:, :, :, 0:D_NOPE])
+            gpsimd_regroup(nope_grouped[:], by_head[:, :, :, 0:D_NOPE])
             wqb_grouped[(r, g)] = (rope_grouped, nope_grouped)
 
         def quantise_wqb(r, g):
@@ -411,8 +433,7 @@ def tile_multiheadlatentattention_pa_kernel(tc, x, Wqa, q_a_norm_w, Wqb, out):
                     in1=table[:, a, :].unsqueeze(1).to_broadcast([P, repeats, N_FREQ // 2]),
                     op=ALU.mult,
                 )
-            last = r == GROUPS - 1 and i == TOK_TILES - 1
-            adder = nc.vector if last else nc.gpsimd
+            adder = nc.vector if r == GROUPS - 1 else nc.gpsimd
             adder.tensor_tensor(
                 out=result[:, :, D_NOPE:D_HEAD].rearrange("p h (i e) -> p h i e", e=2),
                 in0=straight[:].rearrange("p (h i e) -> p h i e", h=GROUP_HEADS, e=2),

@@ -255,23 +255,13 @@ def tile_multiheadlatentattention_pa_kernel(tc, x, Wqa, q_a_norm_w, Wqb, out):
 
         wqb_grouped = {}
 
-        def gpsimd_regroup(grouped, rows):
-            nc.gpsimd.tensor_scalar(
-                out=grouped.rearrange("p (n w) t -> p n w t", n=rows.shape[2]),
-                in0=rows.rearrange("p t n w -> p n w t"),
-                scalar1=1.0,
-                scalar2=0.0,
-                op0=ALU.mult,
-                op1=ALU.add,
-            )
-
         def regroup_wqb(r, g):
             by_head = wqb_tiles[(r, g)][:].rearrange("p t (h f) -> p t h f", f=D_HEAD)
             rope_grouped = grouped_pool.tile(
                 [P, ROPE_COLS, PACK], BF16, tag="grouped_512", align_bytes=64
             )
-            if r == 0:
-                gpsimd_regroup(rope_grouped[:], by_head[:, :, :, D_NOPE:D_HEAD])
+            if r < 2:
+                regroup(nc.vector.tensor_copy, rope_grouped[:], by_head[:, :, :, D_NOPE:D_HEAD])
             else:
                 for h in range(GROUP_HEADS):
                     regroup(
@@ -282,7 +272,7 @@ def tile_multiheadlatentattention_pa_kernel(tc, x, Wqa, q_a_norm_w, Wqb, out):
             nope_grouped = grouped_pool.tile(
                 [P, NOPE_COLS, PACK], BF16, tag="grouped_256", align_bytes=64
             )
-            gpsimd_regroup(nope_grouped[:], by_head[:, :, :, 0:D_NOPE])
+            regroup(nc.scalar.copy, nope_grouped[:], by_head[:, :, :, 0:D_NOPE])
             wqb_grouped[(r, g)] = (rope_grouped, nope_grouped)
 
         def quantise_wqb(r, g):
@@ -433,7 +423,8 @@ def tile_multiheadlatentattention_pa_kernel(tc, x, Wqa, q_a_norm_w, Wqb, out):
                     in1=table[:, a, :].unsqueeze(1).to_broadcast([P, repeats, N_FREQ // 2]),
                     op=ALU.mult,
                 )
-            adder = nc.vector if r == GROUPS - 1 else nc.gpsimd
+            last = r == GROUPS - 1 and i == TOK_TILES - 1
+            adder = nc.vector if last else nc.gpsimd
             adder.tensor_tensor(
                 out=result[:, :, D_NOPE:D_HEAD].rearrange("p h (i e) -> p h i e", e=2),
                 in0=straight[:].rearrange("p (h i e) -> p h i e", h=GROUP_HEADS, e=2),

from contextlib import ExitStack
import math

import concourse.mybir as mybir
from concourse.masks import make_identity

F32 = mybir.dt.float32
BF16 = mybir.dt.bfloat16
I32 = mybir.dt.int32
U32 = mybir.dt.uint32
U8 = mybir.dt.uint8
FP8X4 = mybir.dt.float8_e4m3fn_x4
ALU = mybir.AluOpType
ACT = mybir.ActivationFunctionType

P = 128
PACK = 4
K_PASS = P * PACK
BANK = 512

BATCH, SEQ, D_MODEL, HEADS, D_NOPE, D_ROPE, RANK = 2, 256, 2048, 16, 64, 128, 1536
D_HEAD = D_NOPE + D_ROPE
THETA = 10000.0
EPS = 1e-6
N_FREQ = D_ROPE // 2

TOK_TILES = BATCH * SEQ // P
SEQ_TILES = SEQ // P
X_PASSES = D_MODEL // K_PASS
H_PASSES = RANK // K_PASS
RANK_BANKS = RANK // BANK
GROUP_HEADS = 4
GROUPS = HEADS // GROUP_HEADS
GROUP_COLS = GROUP_HEADS * D_HEAD
ROPE_COLS = GROUP_HEADS * D_ROPE
NOPE_COLS = GROUP_HEADS * D_NOPE
ROUND_MAGIC = 12582912.0

FLOPS = 2 * BATCH * SEQ * (D_MODEL * RANK + RANK * HEADS * D_HEAD)


def regroup(copy, grouped, rows):
    copy(
        out=grouped.rearrange("p (n c i) t -> p n c t i", n=rows.shape[2], i=4),
        in_=rows.rearrange("p t n (c i) -> p n c t i", i=4),
    )


def build_rope_tables(nc, const):
    position_int = const.tile([P, SEQ_TILES], I32)
    nc.gpsimd.iota(position_int[:], pattern=[[P, SEQ_TILES]], base=0, channel_multiplier=1)
    position = const.tile([P, SEQ_TILES], F32)
    nc.vector.tensor_copy(out=position[:], in_=position_int[:])

    freq = const.tile([P, N_FREQ], F32)
    nc.vector.memset(freq[:, 0:1], 1.0)
    for level in range(6):
        span = 1 << level
        nc.vector.tensor_scalar(
            out=freq[:, span : 2 * span],
            in0=freq[:, 0:span],
            scalar1=THETA ** (-span / N_FREQ),
            scalar2=None,
            op0=ALU.mult,
        )

    turns = const.tile([P, 2, SEQ_TILES, N_FREQ], F32)
    for a in range(SEQ_TILES):
        nc.vector.tensor_scalar(
            out=turns[:, 0, a, :],
            in0=freq[:],
            scalar1=position[:, a : a + 1],
            scalar2=1.0 / (2.0 * math.pi),
            op0=ALU.mult,
            op1=ALU.mult,
        )
    nc.vector.tensor_scalar(
        out=turns[:, 1], in0=turns[:, 0], scalar1=0.25, scalar2=None, op0=ALU.add
    )
    whole = const.tile([P, 2, SEQ_TILES, N_FREQ], F32)
    nc.vector.tensor_scalar(
        out=whole[:],
        in0=turns[:],
        scalar1=ROUND_MAGIC,
        scalar2=ROUND_MAGIC,
        op0=ALU.add,
        op1=ALU.subtract,
    )
    part = const.tile([P, 2, SEQ_TILES, N_FREQ], F32)
    nc.vector.tensor_tensor(out=part[:], in0=turns[:], in1=whole[:], op=ALU.subtract)
    trig = const.tile([P, 2, SEQ_TILES, N_FREQ], F32)
    nc.scalar.activation(out=trig[:], in_=part[:], func=ACT.Sin, scale=2.0 * math.pi)
    warm = const.tile([P, 1], F32)
    nc.scalar.sqrt(out=warm[:], in_=freq[:, 0:1])

    sin_pairs = trig[:, 0].rearrange("p a (i e) -> p a i e", e=2)
    neg_sin_even = const.tile([P, SEQ_TILES, N_FREQ // 2], F32)
    nc.vector.tensor_scalar(
        out=neg_sin_even[:], in0=sin_pairs[:, :, :, 0], scalar1=-1.0, scalar2=None, op0=ALU.mult
    )
    sin_odd = const.tile([P, SEQ_TILES, N_FREQ // 2], F32)
    nc.vector.tensor_copy(out=sin_odd[:], in_=sin_pairs[:, :, :, 1])
    return trig[:, 1], neg_sin_even, sin_odd


def tile_multiheadlatentattention_pa_kernel(tc, x, Wqa, q_a_norm_w, Wqb, out):
    nc = tc.nc
    x_rows = x.flatten_outer_dims()

    with ExitStack() as ctx:
        const = ctx.enter_context(tc.tile_pool(name="const", bufs=1))
        keep = ctx.enter_context(tc.tile_pool(name="keep", bufs=1))
        grouped_pool = ctx.enter_context(tc.tile_pool(name="grouped", bufs=4))
        norm_pool = ctx.enter_context(tc.tile_pool(name="norm", bufs=2))
        psum = ctx.enter_context(tc.psum_pool(name="psum", bufs=8))

        x_codes = keep.tile([P, TOK_TILES, X_PASSES * P], U32, align_bytes=64)
        x_scales = keep.tile([P, TOK_TILES, X_PASSES * P], U8, align_bytes=64)
        wqa_codes = keep.tile([P, X_PASSES, RANK], U32, align_bytes=64)
        wqa_scales = keep.tile([P, X_PASSES, RANK], U8, align_bytes=64)
        h_codes = keep.tile([P, TOK_TILES, H_PASSES, P], U32, align_bytes=64)
        h_scales = keep.tile([P, TOK_TILES, H_PASSES, P], U8, align_bytes=64)
        rope_codes = keep.tile([P, GROUPS, H_PASSES, ROPE_COLS], U32, align_bytes=64)
        rope_scales = keep.tile([P, GROUPS, H_PASSES, ROPE_COLS], U8, align_bytes=64)
        nope_codes = keep.tile([P, GROUPS, H_PASSES, NOPE_COLS], U32, align_bytes=64)
        nope_scales = keep.tile([P, GROUPS, H_PASSES, NOPE_COLS], U8, align_bytes=64)

        ident_f32 = const.tile([P, P], F32)
        make_identity(nc, ident_f32[:])
        ident_bf16 = const.tile([P, P], BF16)
        make_identity(nc, ident_bf16[:])
        cos_table, neg_sin_even, sin_odd = build_rope_tables(nc, const)

        gain_row = const.tile([P, RANK], BF16)
        nc.vector.memset(gain_row[:].bitcast(I32), 0)
        nc.sync.dma_start(out=gain_row[0:1, :], in_=q_a_norm_w.unsqueeze(0))
        ones = const.tile([P, P], BF16)
        nc.vector.memset(ones[:], 1.0)
        gain = const.tile([P, RANK], BF16)
        for n in range(RANK_BANKS):
            cols = slice(n * BANK, (n + 1) * BANK)
            gain_bank = psum.tile([P, BANK], F32, tag="bank")
            nc.tensor.matmul(
                out=gain_bank[:], lhsT=ones[:], rhs=gain_row[:, cols], start=True, stop=True
            )
            nc.vector.tensor_copy(out=gain[:, cols], in_=gain_bank[:])

        def quantise(grouped, codes, scales):
            nc.vector.quantize_mx(
                out=codes.bitcast(FP8X4), scales=scales, in_=grouped.rearrange("p c t -> p (c t)")
            )

        def new_c_banks(i):
            return [
                psum.tile([P, BANK], F32, tag="bank", name="c_%d_%d" % (i, n))
                for n in range(RANK_BANKS)
            ]

        def first_matmul(c_banks, i, g, banks):
            for n in banks:
                nc.tensor.matmul_mx(
                    out=c_banks[n][:],
                    lhsT=x_codes[:, i, g * P : (g + 1) * P].bitcast(FP8X4),
                    lhsT_scale=x_scales[:, i, g * P : (g + 1) * P],
                    rhs=wqa_codes[:, g, n * BANK : (n + 1) * BANK].bitcast(FP8X4),
                    rhs_scale=wqa_scales[:, g, n * BANK : (n + 1) * BANK],
                    start=(g == 0),
                    stop=(g == X_PASSES - 1),
                )

        c_banks = {}
        with tc.tile_pool(name="x", bufs=TOK_TILES) as x_pool, tc.tile_pool(
            name="wqa_raw", bufs=X_PASSES
        ) as wqa_pool:
            def load_x(i):
                x_sb = x_pool.tile([P, D_MODEL], BF16)
                nc.sync.dma_start(out=x_sb[:], in_=x_rows[i * P : (i + 1) * P, :])
                return x_sb

            x_tiles = [load_x(i) for i in range(2)]
            wqa_tiles = []
            for g in range(X_PASSES):
                wqa_raw = wqa_pool.tile([P, PACK, RANK], BF16)
                nc.sync.dma_start(
                    out=wqa_raw[:].rearrange("p (u e) c -> p u e c", e=2),
                    in_=Wqa[g * K_PASS : (g + 1) * K_PASS, :].rearrange(
                        "(u q e) c -> q u e c", u=2, e=2
                    ),
                )
                wqa_tiles.append(wqa_raw)
            x_tiles.extend([load_x(i) for i in range(2, TOK_TILES)])

            def quantise_x(i):
                x_words = x_tiles[i][:].bitcast(F32)
                x_grouped = x_pool.tile([P, D_MODEL], BF16, bufs=2, align_bytes=64)
                x_grouped_words = x_grouped[:].bitcast(F32).rearrange(
                    "p (g r u) -> p g r u", g=X_PASSES, u=2
                )
                for half in range(2):
                    x_t = psum.tile([P, 2, 2, P], F32, tag="bank")
                    for gg in range(2):
                        for u in range(2):
                            first = ((2 * half + gg) * 2 + u) * P
                            nc.tensor.transpose(
                                x_t[:, gg, u, :], x_words[:, first : first + P], ident_f32[:]
                            )
                    nc.scalar.copy(
                        out=x_grouped_words[:, 2 * half : 2 * half + 2],
                        in_=x_t[:].rearrange("p g u r -> p g r u"),
                    )
                nc.vector.quantize_mx(
                    out=x_codes[:, i, :].bitcast(FP8X4), scales=x_scales[:, i, :], in_=x_grouped[:]
                )

            for i in range(2):
                quantise_x(i)

            for i in range(2):
                c_banks[i] = new_c_banks(i)
            for g in range(X_PASSES):
                blocks = []
                for n in range(RANK_BANKS):
                    on_vector = (g * RANK_BANKS + n) % 2 == 1
                    wqa_grouped = grouped_pool.tile(
                        [P, BANK, PACK], BF16, tag="grouped_512", align_bytes=64
                    )
                    regroup(
                        nc.vector.tensor_copy if on_vector else nc.scalar.copy,
                        wqa_grouped[:],
                        wqa_tiles[g][:, :, n * BANK : (n + 1) * BANK].unsqueeze(2),
                    )
                    blocks.append(wqa_grouped)
                for n in range(RANK_BANKS):
                    cols = slice(n * BANK, (n + 1) * BANK)
                    quantise(blocks[n][:], wqa_codes[:, g, cols], wqa_scales[:, g, cols])
                for i in range(2):
                    first_matmul(c_banks[i], i, g, range(RANK_BANKS))
            for i in range(2, TOK_TILES):
                quantise_x(i)

        wqb_pool = ctx.enter_context(tc.tile_pool(name="wqb_raw", bufs=6, reuse_waits="tile"))
        rope_pool = ctx.enter_context(tc.tile_pool(name="rope", bufs=3, reuse_waits="tile"))

        wqb_tiles = {}
        for r in range(GROUPS):
            for g in range(H_PASSES):
                wqb_raw = wqb_pool.tile([P, PACK, GROUP_COLS], BF16)
                nc.sync.dma_start(
                    out=wqb_raw[:],
                    in_=Wqb[
                        g * K_PASS : (g + 1) * K_PASS, r * GROUP_COLS : (r + 1) * GROUP_COLS
                    ].rearrange("(t p) c -> p t c", p=P),
                )
                wqb_tiles[(r, g)] = wqb_raw

        wqb_grouped = {}

        def regroup_wqb(r, g):
            by_head = wqb_tiles[(r, g)][:].rearrange("p t (h f) -> p t h f", f=D_HEAD)
            rope_grouped = grouped_pool.tile(
                [P, ROPE_COLS, PACK], BF16, tag="grouped_512", align_bytes=64
            )
            if r < 2:
                regroup(nc.vector.tensor_copy, rope_grouped[:], by_head[:, :, :, D_NOPE:D_HEAD])
            else:
                for h in range(GROUP_HEADS):
                    regroup(
                        nc.scalar.copy,
                        rope_grouped[:, h * D_ROPE : (h + 1) * D_ROPE, :],
                        by_head[:, :, h : h + 1, D_NOPE:D_HEAD],
                    )
            nope_grouped = grouped_pool.tile(
                [P, NOPE_COLS, PACK], BF16, tag="grouped_256", align_bytes=64
            )
            regroup(nc.scalar.copy, nope_grouped[:], by_head[:, :, :, 0:D_NOPE])
            wqb_grouped[(r, g)] = (rope_grouped, nope_grouped)

        def quantise_wqb(r, g):
            rope_grouped, nope_grouped = wqb_grouped[(r, g)]
            quantise(rope_grouped[:], rope_codes[:, r, g, :], rope_scales[:, r, g, :])
            quantise(nope_grouped[:], nope_codes[:, r, g, :], nope_scales[:, r, g, :])

        sum_sq = {}
        rstd = {}
        h_rows = {}
        h_grouped = {}

        def square(i, n):
            if n == 0:
                sum_sq[i] = norm_pool.tile([P, RANK_BANKS], F32, name="sum_sq")
            squares = norm_pool.tile([P, BANK], BF16)
            nc.scalar.activation(
                out=squares[:],
                in_=c_banks[i][n][:],
                func=ACT.Square,
                accum_out=sum_sq[i][:, n : n + 1],
            )

        def mean_square(i):
            rstd[i] = norm_pool.tile([P, 1], F32, name="rstd")
            nc.vector.tensor_reduce(
                out=rstd[i][:], in_=sum_sq[i][:], axis=mybir.AxisListType.X, op=ALU.add
            )
            nc.vector.tensor_scalar(
                out=rstd[i][:],
                in0=rstd[i][:],
                scalar1=1.0 / RANK,
                scalar2=EPS,
                op0=ALU.mult,
                op1=ALU.add,
            )

        def scale_and_transpose(i, n):
            if n == 0:
                h_rows[i] = norm_pool.tile([P, RANK], BF16, name="h_rows")
            cols = slice(n * BANK, (n + 1) * BANK)
            nc.vector.scalar_tensor_tensor(
                out=h_rows[i][:, cols],
                in0=c_banks[i][n][:],
                scalar=rstd[i][:, 0:1],
                in1=gain[:, cols],
                op0=ALU.mult,
                op1=ALU.mult,
            )
            h_t = psum.tile([P, PACK, P], BF16, tag="bank")
            for t in range(PACK):
                first = n * K_PASS + t * P
                nc.tensor.transpose(h_t[:, t, :], h_rows[i][:, first : first + P], ident_bf16[:])
            h_grouped[(i, n)] = h_t

        def copy_h(i, g):
            h_t = h_grouped[(i, g)]
            h_words = norm_pool.tile([P, P, PACK], BF16, bufs=6, align_bytes=64)
            nc.scalar.copy(out=h_words[:], in_=h_t[:].rearrange("p t r -> p r t"))
            h_grouped[(i, g)] = h_words

        def quantise_h(i, g):
            quantise(h_grouped[(i, g)][:], h_codes[:, i, g, :], h_scales[:, i, g, :])

        def norm_front(i):
            for n in range(RANK_BANKS):
                square(i, n)

        def move_c_to_sbuf(i):
            c_rows = norm_pool.tile([P, RANK], F32)
            for n in range(RANK_BANKS):
                nc.vector.tensor_copy(out=c_rows[:, n * BANK : (n + 1) * BANK], in_=c_banks[i][n][:])
            c_banks[i] = [c_rows[:, n * BANK : (n + 1) * BANK] for n in range(RANK_BANKS)]

        def norm_middle(i):
            mean_square(i)
            nc.scalar.sqrt(out=rstd[i][:], in_=rstd[i][:])
            nc.vector.reciprocal(out=rstd[i][:], in_=rstd[i][:])
            for n in range(RANK_BANKS):
                scale_and_transpose(i, n)

        def norm_back(i):
            for g in range(H_PASSES):
                copy_h(i, g)
            for g in range(H_PASSES):
                quantise_h(i, g)

        for i in range(2):
            norm_front(i)
            move_c_to_sbuf(i)
        for i in range(2, TOK_TILES):
            c_banks[i] = new_c_banks(i)
            for n in range(RANK_BANKS):
                for g in range(X_PASSES):
                    first_matmul(c_banks[i], i, g, [n])
        for i in range(2):
            norm_middle(i)
        for i in range(2):
            norm_back(i)
        for i in range(2, TOK_TILES):
            norm_front(i)
        for i in range(2, TOK_TILES):
            norm_middle(i)
        for i in range(2, TOK_TILES):
            norm_back(i)
        for g in range(H_PASSES):
            regroup_wqb(0, g)
        for g in range(H_PASSES):
            quantise_wqb(0, g)

        def second_matmul_and_rope(r, i):
            rope_q = psum.tile([P, ROPE_COLS], F32, tag="bank")
            nope_q = psum.tile([P, NOPE_COLS], F32, tag="bank")
            for g in range(H_PASSES):
                for q_bank, codes, scales in (
                    (rope_q, rope_codes, rope_scales),
                    (nope_q, nope_codes, nope_scales),
                ):
                    nc.tensor.matmul_mx(
                        out=q_bank[:],
                        lhsT=h_codes[:, i, g, :].bitcast(FP8X4),
                        lhsT_scale=h_scales[:, i, g, :],
                        rhs=codes[:, r, g, :].bitcast(FP8X4),
                        rhs_scale=scales[:, r, g, :],
                        start=(g == 0),
                        stop=(g == H_PASSES - 1),
                    )

            a = i % SEQ_TILES
            result = rope_pool.tile([P, GROUP_HEADS, D_HEAD], F32, bufs=6)
            nc.scalar.copy(
                out=result[:, :, 0:D_NOPE], in_=nope_q[:].rearrange("p (h f) -> p h f", f=D_NOPE)
            )
            repeats = ROPE_COLS // N_FREQ
            straight = rope_pool.tile([P, ROPE_COLS], F32, bufs=5)
            nc.vector.tensor_tensor(
                out=straight[:].rearrange("p (m j) -> p m j", j=N_FREQ),
                in0=rope_q[:].rearrange("p (m j) -> p m j", j=N_FREQ),
                in1=cos_table[:, a, :].unsqueeze(1).to_broadcast([P, repeats, N_FREQ]),
                op=ALU.mult,
            )
            crossed = rope_pool.tile([P, 2, ROPE_COLS // 2], F32, bufs=5)
            pairs = rope_q[:].rearrange("p (m i e) -> p m i e", i=N_FREQ // 2, e=2)
            for e, table in ((0, neg_sin_even), (1, sin_odd)):
                nc.vector.tensor_tensor(
                    out=crossed[:, e, :].rearrange("p (m i) -> p m i", i=N_FREQ // 2),
                    in0=pairs[:, :, :, 1 - e],
                    in1=table[:, a, :].unsqueeze(1).to_broadcast([P, repeats, N_FREQ // 2]),
                    op=ALU.mult,
                )
            last = r == GROUPS - 1 and i == TOK_TILES - 1
            adder = nc.vector if last else nc.gpsimd
            adder.tensor_tensor(
                out=result[:, :, D_NOPE:D_HEAD].rearrange("p h (i e) -> p h i e", e=2),
                in0=straight[:].rearrange("p (h i e) -> p h i e", h=GROUP_HEADS, e=2),
                in1=crossed[:].rearrange("p e (h i) -> p h i e", h=GROUP_HEADS),
                op=ALU.add,
            )
            nc.sync.dma_start(
                out=out[
                    i // SEQ_TILES, r * GROUP_HEADS : (r + 1) * GROUP_HEADS, a * P : (a + 1) * P, :
                ].rearrange("h s f -> s h f"),
                in_=result[:],
            )

        for r in range(GROUPS):
            for i in range(TOK_TILES):
                if r + 1 < GROUPS and i < H_PASSES:
                    regroup_wqb(r + 1, i)
                second_matmul_and_rope(r, i)
                if r + 1 < GROUPS and i > 0:
                    quantise_wqb(r + 1, i - 1)
